import numpy as np
import ml_dtypes


def mxq(x, axis, fmt="e4m3"):
    dtype, down = {"e4m3": (ml_dtypes.float8_e4m3fn, 7), "e5m2": (ml_dtypes.float8_e5m2, 14)}[fmt]
    v = np.moveaxis(np.asarray(x, np.float32).astype(ml_dtypes.bfloat16).astype(np.float64), axis, -1)
    blocks = v.reshape(v.shape[:-1] + (-1, 32))
    amax = np.abs(blocks).max(-1, keepdims=True)
    byte = np.maximum(np.where(amax > 0, np.frexp(amax)[1] - 1 + 127, 0) - down, 1)
    scale = np.exp2(byte - 127.0)
    codes = (blocks / scale).astype(np.float32).astype(dtype).astype(np.float64)
    return np.moveaxis((codes * scale).reshape(v.shape), -1, axis)


WIDE = False


def mx_kscale(k):
    if not WIDE:
        return np.ones(k)
    levels = np.array([10, -10, 5, -5, 0])
    a = np.random.permutation(np.resize(levels, k // 512 * 4)).reshape(k // 512, 4)
    idx = np.arange(k)
    return np.exp2(a[idx // 512, idx % 128 // 32])


BF16 = ml_dtypes.bfloat16


def bf(x):
    return np.asarray(x, np.float32).astype(BF16)


def f64(x):
    return np.asarray(x).astype(np.float64)


N, IN, HID, OUT, NB = 512, 512, 384, 256, 64
EPS = 1e-8


def draw_adj():
    r = np.exp(0.5 * np.random.standard_normal(N))
    u = np.random.uniform(size=(N, N)) * (np.random.uniform(size=(N, N)) < NB / N)
    return u * r[:, None] * r[None, :]


def setup_inputs():
    t = mx_kscale(IN)
    return {"x": bf(np.random.standard_normal((N, IN)) * 0.25 * np.sqrt(NB) * t[None, :]),
            "adj": bf(draw_adj()),
            "W1": bf(np.random.standard_normal((HID, IN)) * 3.0 / np.sqrt(IN) / t[None, :]),
            "b1": bf(np.random.standard_normal(HID) * 0.3)}


def reference(x, adj, W1, b1):
    a = f64(adj)
    deg = a.sum(axis=1)
    d = 1.0 / np.sqrt(deg + EPS)
    norm_adj = d[:, None] * a * d[None, :]
    agg = mxq(norm_adj, 1, "e4m3") @ mxq(f64(x), 0, "e4m3")
    return np.maximum((mxq(agg, 1, "e4m3") @ mxq(f64(W1), 1, "e4m3").T) + f64(b1), 0.0)

@@ -1,0 +1,150 @@
+from contextlib import ExitStack
+
+from concourse import mybir
+from concourse.masks import make_identity
+
+F32 = mybir.dt.float32
+BF16 = mybir.dt.bfloat16
+U32 = mybir.dt.uint32
+U8 = mybir.dt.uint8
+FP8X4 = mybir.dt.float8_e4m3fn_x4
+ACT = mybir.ActivationFunctionType
+ALU = mybir.AluOpType
+AXIS = mybir.AxisListType
+
+P = 128
+PACK = 4
+NODES = 512
+FEATS = 512
+HIDDEN = 384
+EPS = 1e-8
+NODE_TILES = NODES // P
+HIDDEN_TILES = HIDDEN // P
+HIDDEN_PASSES = ((0, 256), (256, 128))
+
+FLOPS = 2 * NODES * NODES * FEATS + 2 * NODES * FEATS * HIDDEN
+
+
+def tile_simplegcn_pa_s_kernel(tc, x, adj, W1, b1, out):
+    nc = tc.nc
+    with ExitStack() as ctx:
+        keep = ctx.enter_context(tc.tile_pool(name="keep", bufs=1))
+        work = ctx.enter_context(tc.tile_pool(name="work", bufs=2))
+        psum = ctx.enter_context(tc.psum_pool(name="psum", bufs=2))
+
+        adj_sb = keep.tile([P, NODE_TILES, NODES], BF16)
+        for a in range(NODE_TILES):
+            nc.sync.dma_start(out=adj_sb[:, a, :], in_=adj[a * P : (a + 1) * P, :])
+        x_sb = keep.tile([P, PACK, FEATS], BF16)
+        nc.sync.dma_start(out=x_sb[:], in_=x.rearrange("(t p) f -> p t f", p=P))
+        w_sb = keep.tile([P, HIDDEN_TILES, FEATS], BF16)
+        nc.sync.dma_start(out=w_sb[:], in_=W1.rearrange("(c p) f -> p c f", p=P))
+        bias_sb = keep.tile([P, HIDDEN], BF16)
+        nc.sync.dma_start(out=bias_sb[:], in_=b1.partition_broadcast(P))
+
+        ident_f32 = keep.tile([P, P], F32)
+        make_identity(nc, ident_f32[:])
+        ident_bf16 = keep.tile([P, P], BF16)
+        make_identity(nc, ident_bf16[:])
+        warm = keep.tile([P, 1], F32)
+        nc.vector.memset(warm[:], 1.0)
+        nc.scalar.activation(out=warm[:], in_=warm[:], func=ACT.Sqrt)
+
+        deg = keep.tile([P, NODE_TILES, 8], F32)
+        root = keep.tile([P, NODE_TILES], F32)
+        d_col = keep.tile([P, NODE_TILES], F32)
+        unread = keep.tile([P, NODE_TILES, NODES], BF16)
+        rows_scaled = keep.tile([P, NODE_TILES, NODES], F32)
+        for a in range(NODE_TILES):
+            if a % 2 == 0:
+                nc.vector.tensor_reduce(out=deg[:, a, 0:1], in_=adj_sb[:, a, :], axis=AXIS.X, op=ALU.add)
+            else:
+                nc.scalar.activation(
+                    out=unread[:, a, :], in_=adj_sb[:, a, :], func=ACT.Copy, accum_out=deg[:, a, 0:1]
+                )
+            nc.scalar.activation(out=root[:, a : a + 1], in_=deg[:, a, 0:1], func=ACT.Sqrt, bias=EPS)
+            nc.vector.reciprocal(out=d_col[:, a : a + 1], in_=root[:, a : a + 1])
+            nc.vector.tensor_scalar_mul(
+                out=rows_scaled[:, a, :], in0=adj_sb[:, a, :], scalar1=d_col[:, a : a + 1]
+            )
+
+        x_grouped = keep.tile([P, FEATS, PACK], BF16, align_bytes=64)
+        x_codes = keep.tile([P, FEATS], U32, align_bytes=64)
+        x_scales = keep.tile([P, FEATS], U8, align_bytes=64)
+        nc.scalar.copy(out=x_grouped[:], in_=x_sb[:].rearrange("p t f -> p f t"))
+        nc.vector.quantize_mx(
+            out=x_codes[:].bitcast(FP8X4),
+            scales=x_scales[:],
+            in_=x_grouped[:].rearrange("p f t -> p (f t)"),
+        )
+
+        adj_grouped = keep.tile([P, NODE_TILES, P, PACK], BF16, align_bytes=64)
+        adj_codes = keep.tile([P, NODE_TILES, P], U32, align_bytes=64)
+        adj_scales = keep.tile([P, NODE_TILES, P], U8, align_bytes=64)
+        for a in range(NODE_TILES):
+            adjT_ps = psum.tile([P, PACK, P], F32)
+            for t in range(PACK):
+                nc.tensor.transpose(adjT_ps[:, t, :], rows_scaled[:, a, t * P : (t + 1) * P], ident_f32[:])
+            nc.vector.tensor_tensor(
+                out=adj_grouped[:, a],
+                in0=adjT_ps[:].rearrange("p t i -> p i t"),
+                in1=d_col[:].unsqueeze(1).to_broadcast([P, P, PACK]),
+                op=ALU.mult,
+            )
+            nc.vector.quantize_mx(
+                out=adj_codes[:, a, :].bitcast(FP8X4),
+                scales=adj_scales[:, a, :],
+                in_=adj_grouped[:, a].rearrange("p i t -> p (i t)"),
+            )
+
+        w_grouped = keep.tile([P, HIDDEN_TILES, P, PACK], BF16, align_bytes=64)
+        w_codes = keep.tile([P, HIDDEN], U32, align_bytes=64)
+        w_scales = keep.tile([P, HIDDEN], U8, align_bytes=64)
+        for c in range(HIDDEN_TILES):
+            wT_ps = psum.tile([P, PACK, P], BF16)
+            for t in range(PACK):
+                nc.tensor.transpose(wT_ps[:, t, :], w_sb[:, c, t * P : (t + 1) * P], ident_bf16[:])
+            nc.scalar.copy(out=w_grouped[:, c], in_=wT_ps[:].rearrange("p t h -> p h t"))
+            nc.vector.quantize_mx(
+                out=w_codes[:, c * P : (c + 1) * P].bitcast(FP8X4),
+                scales=w_scales[:, c * P : (c + 1) * P],
+                in_=w_grouped[:, c].rearrange("p h t -> p (h t)"),
+            )
+
+        for a in range(NODE_TILES):
+            aggT_ps = psum.tile([P, PACK, P], F32)
+            for t in range(PACK):
+                nc.tensor.matmul_mx(
+                    out=aggT_ps[:, t, :],
+                    lhsT=x_codes[:, t * P : (t + 1) * P].bitcast(FP8X4),
+                    lhsT_scale=x_scales[:, t * P : (t + 1) * P],
+                    rhs=adj_codes[:, a, :].bitcast(FP8X4),
+                    rhs_scale=adj_scales[:, a, :],
+                    start=True,
+                    stop=True,
+                )
+            agg_grouped = work.tile([P, P, PACK], BF16, align_bytes=64)
+            agg_codes = work.tile([P, P], U32, align_bytes=64)
+            agg_scales = work.tile([P, P], U8, align_bytes=64)
+            nc.scalar.copy(out=agg_grouped[:], in_=aggT_ps[:].rearrange("p t i -> p i t"))
+            nc.vector.quantize_mx(
+                out=agg_codes[:].bitcast(FP8X4),
+                scales=agg_scales[:],
+                in_=agg_grouped[:].rearrange("p i t -> p (i t)"),
+            )
+            out_ps = psum.tile([P, HIDDEN], F32)
+            for first, width in HIDDEN_PASSES:
+                nc.tensor.matmul_mx(
+                    out=out_ps[:, first : first + width],
+                    lhsT=agg_codes[:].bitcast(FP8X4),
+                    lhsT_scale=agg_scales[:],
+                    rhs=w_codes[:, first : first + width].bitcast(FP8X4),
+                    rhs_scale=w_scales[:, first : first + width],
+                    start=True,
+                    stop=True,
+                )
+            biased = work.tile([P, HIDDEN], F32)
+            nc.vector.tensor_tensor(out=biased[:], in0=out_ps[:], in1=bias_sb[:], op=ALU.add)
+            result = work.tile([P, HIDDEN], F32)
+            nc.scalar.activation(out=result[:], in_=biased[:], func=ACT.Relu)
+            nc.sync.dma_start(out=out[a * P : (a + 1) * P, :], in_=result[:])

@@ -28,91 +28,78 @@ FLOPS = 2 * NODES * NODES * FEATS + 2 * NODES * FEATS * HIDDEN
 def tile_simplegcn_pa_s_kernel(tc, x, adj, W1, b1, out):
     nc = tc.nc
     with ExitStack() as ctx:
+        ctx.enter_context(tc.manual_schedule())
         keep = ctx.enter_context(tc.tile_pool(name="keep", bufs=1))
-        work = ctx.enter_context(tc.tile_pool(name="work", bufs=2))
-        psum = ctx.enter_context(tc.psum_pool(name="psum", bufs=2))
+        psum = ctx.enter_context(tc.psum_pool(name="psum", bufs=8))
 
         adj_sb = keep.tile([P, NODE_TILES, NODES], BF16)
-        for a in range(NODE_TILES):
-            nc.sync.dma_start(out=adj_sb[:, a, :], in_=adj[a * P : (a + 1) * P, :])
         x_sb = keep.tile([P, PACK, FEATS], BF16)
-        nc.sync.dma_start(out=x_sb[:], in_=x.rearrange("(t p) f -> p t f", p=P))
         w_sb = keep.tile([P, HIDDEN_TILES, FEATS], BF16)
-        nc.sync.dma_start(out=w_sb[:], in_=W1.rearrange("(c p) f -> p c f", p=P))
         bias_sb = keep.tile([P, HIDDEN], BF16)
-        nc.sync.dma_start(out=bias_sb[:], in_=b1.partition_broadcast(P))
-
         ident_f32 = keep.tile([P, P], F32)
-        make_identity(nc, ident_f32[:])
         ident_bf16 = keep.tile([P, P], BF16)
-        make_identity(nc, ident_bf16[:])
         warm = keep.tile([P, 1], F32)
-        nc.vector.memset(warm[:], 1.0)
-        nc.scalar.activation(out=warm[:], in_=warm[:], func=ACT.Sqrt)
-
         deg = keep.tile([P, NODE_TILES, 8], F32)
         root = keep.tile([P, NODE_TILES], F32)
         d_col = keep.tile([P, NODE_TILES], F32)
         unread = keep.tile([P, NODE_TILES, NODES], BF16)
         rows_scaled = keep.tile([P, NODE_TILES, NODES], F32)
-        for a in range(NODE_TILES):
+        x_grouped = keep.tile([P, FEATS, PACK], BF16, align_bytes=64)
+        x_codes = keep.tile([P, FEATS], U32, align_bytes=64)
+        x_scales = keep.tile([P, FEATS], U8, align_bytes=64)
+        adj_grouped = keep.tile([P, NODE_TILES, P, PACK], BF16, align_bytes=64)
+        adj_codes = keep.tile([P, NODE_TILES, P], U32, align_bytes=64)
+        adj_scales = keep.tile([P, NODE_TILES, P], U8, align_bytes=64)
+        w_grouped = keep.tile([P, HIDDEN_TILES, P, PACK], BF16, align_bytes=64)
+        w_codes = keep.tile([P, HIDDEN], U32, align_bytes=64)
+        w_scales = keep.tile([P, HIDDEN], U8, align_bytes=64)
+        agg_grouped = keep.tile([P, NODE_TILES, P, PACK], BF16, align_bytes=64)
+        agg_codes = keep.tile([P, NODE_TILES, P], U32, align_bytes=64)
+        agg_scales = keep.tile([P, NODE_TILES, P], U8, align_bytes=64)
+        biased = keep.tile([P, NODE_TILES, HIDDEN], F32)
+        result = keep.tile([P, NODE_TILES, HIDDEN], F32)
+        banks = {}
+
+        def row_sum(a):
             if a % 2 == 0:
                 nc.vector.tensor_reduce(out=deg[:, a, 0:1], in_=adj_sb[:, a, :], axis=AXIS.X, op=ALU.add)
             else:
                 nc.scalar.activation(
                     out=unread[:, a, :], in_=adj_sb[:, a, :], func=ACT.Copy, accum_out=deg[:, a, 0:1]
                 )
-            nc.scalar.activation(out=root[:, a : a + 1], in_=deg[:, a, 0:1], func=ACT.Sqrt, bias=EPS)
-            nc.vector.reciprocal(out=d_col[:, a : a + 1], in_=root[:, a : a + 1])
-            nc.vector.tensor_scalar_mul(
-                out=rows_scaled[:, a, :], in0=adj_sb[:, a, :], scalar1=d_col[:, a : a + 1]
+
+        def group_x(half):
+            cols = slice(half * FEATS // 2, (half + 1) * FEATS // 2)
+            nc.vector.tensor_copy(out=x_grouped[:, cols, :], in_=x_sb[:, :, cols].rearrange("p t f -> p f t"))
+
+        def quantise(codes, scales, grouped):
+            nc.vector.quantize_mx(out=codes.bitcast(FP8X4), scales=scales, in_=grouped)
+
+        def scale_and_transpose_rows(a):
+            nc.scalar.activation(
+                out=rows_scaled[:, a, :], in_=adj_sb[:, a, :], func=ACT.Copy, scale=d_col[:, a : a + 1]
             )
-
-        x_grouped = keep.tile([P, FEATS, PACK], BF16, align_bytes=64)
-        x_codes = keep.tile([P, FEATS], U32, align_bytes=64)
-        x_scales = keep.tile([P, FEATS], U8, align_bytes=64)
-        nc.scalar.copy(out=x_grouped[:], in_=x_sb[:].rearrange("p t f -> p f t"))
-        nc.vector.quantize_mx(
-            out=x_codes[:].bitcast(FP8X4),
-            scales=x_scales[:],
-            in_=x_grouped[:].rearrange("p f t -> p (f t)"),
-        )
-
-        adj_grouped = keep.tile([P, NODE_TILES, P, PACK], BF16, align_bytes=64)
-        adj_codes = keep.tile([P, NODE_TILES, P], U32, align_bytes=64)
-        adj_scales = keep.tile([P, NODE_TILES, P], U8, align_bytes=64)
-        for a in range(NODE_TILES):
-            adjT_ps = psum.tile([P, PACK, P], F32)
+            adjT_ps = psum.tile([P, PACK, P], F32, tag="bank")
             for t in range(PACK):
                 nc.tensor.transpose(adjT_ps[:, t, :], rows_scaled[:, a, t * P : (t + 1) * P], ident_f32[:])
+            banks["adjT", a] = adjT_ps
+
+        def finish_norm_adj(a):
             nc.vector.tensor_tensor(
                 out=adj_grouped[:, a],
-                in0=adjT_ps[:].rearrange("p t i -> p i t"),
+                in0=banks["adjT", a][:].rearrange("p t i -> p i t"),
                 in1=d_col[:].unsqueeze(1).to_broadcast([P, P, PACK]),
                 op=ALU.mult,
             )
-            nc.vector.quantize_mx(
-                out=adj_codes[:, a, :].bitcast(FP8X4),
-                scales=adj_scales[:, a, :],
-                in_=adj_grouped[:, a].rearrange("p i t -> p (i t)"),
-            )
 
-        w_grouped = keep.tile([P, HIDDEN_TILES, P, PACK], BF16, align_bytes=64)
-        w_codes = keep.tile([P, HIDDEN], U32, align_bytes=64)
-        w_scales = keep.tile([P, HIDDEN], U8, align_bytes=64)
-        for c in range(HIDDEN_TILES):
-            wT_ps = psum.tile([P, PACK, P], BF16)
+        def transpose_w(c):
+            wT_ps = psum.tile([P, PACK, P], BF16, tag="bank")
             for t in range(PACK):
                 nc.tensor.transpose(wT_ps[:, t, :], w_sb[:, c, t * P : (t + 1) * P], ident_bf16[:])
-            nc.scalar.copy(out=w_grouped[:, c], in_=wT_ps[:].rearrange("p t h -> p h t"))
-            nc.vector.quantize_mx(
-                out=w_codes[:, c * P : (c + 1) * P].bitcast(FP8X4),
-                scales=w_scales[:, c * P : (c + 1) * P],
-                in_=w_grouped[:, c].rearrange("p h t -> p (h t)"),
-            )
+            banks["wT", c] = wT_ps
 
-        for a in range(NODE_TILES):
-            aggT_ps = psum.tile([P, PACK, P], F32)
+        def first_matmul(a):
+            aggT_ps = psum.tile([P, PACK, P], F32, tag="bank")
             for t in range(PACK):
                 nc.tensor.matmul_mx(
                     out=aggT_ps[:, t, :],
@@ -123,28 +110,75 @@ def tile_simplegcn_pa_s_kernel(tc, x, adj, W1, b1, out):
                     start=True,
                     stop=True,
                 )
-            agg_grouped = work.tile([P, P, PACK], BF16, align_bytes=64)
-            agg_codes = work.tile([P, P], U32, align_bytes=64)
-            agg_scales = work.tile([P, P], U8, align_bytes=64)
-            nc.scalar.copy(out=agg_grouped[:], in_=aggT_ps[:].rearrange("p t i -> p i t"))
-            nc.vector.quantize_mx(
-                out=agg_codes[:].bitcast(FP8X4),
-                scales=agg_scales[:],
-                in_=agg_grouped[:].rearrange("p i t -> p (i t)"),
-            )
-            out_ps = psum.tile([P, HIDDEN], F32)
+            nc.scalar.copy(out=agg_grouped[:, a], in_=aggT_ps[:].rearrange("p t i -> p i t"))
+
+        def second_matmul(a):
+            out_ps = psum.tile([P, HIDDEN], F32, tag="bank")
             for first, width in HIDDEN_PASSES:
                 nc.tensor.matmul_mx(
                     out=out_ps[:, first : first + width],
-                    lhsT=agg_codes[:].bitcast(FP8X4),
-                    lhsT_scale=agg_scales[:],
+                    lhsT=agg_codes[:, a, :].bitcast(FP8X4),
+                    lhsT_scale=agg_scales[:, a, :],
                     rhs=w_codes[:, first : first + width].bitcast(FP8X4),
                     rhs_scale=w_scales[:, first : first + width],
                     start=True,
                     stop=True,
                 )
-            biased = work.tile([P, HIDDEN], F32)
-            nc.vector.tensor_tensor(out=biased[:], in0=out_ps[:], in1=bias_sb[:], op=ALU.add)
-            result = work.tile([P, HIDDEN], F32)
-            nc.scalar.activation(out=result[:], in_=biased[:], func=ACT.Relu)
-            nc.sync.dma_start(out=out[a * P : (a + 1) * P, :], in_=result[:])
+            banks["out", a] = out_ps
+
+        def finish_out(a):
+            nc.vector.tensor_tensor(out=biased[:, a, :], in0=banks["out", a][:], in1=bias_sb[:], op=ALU.add)
+            nc.gpsimd.tensor_scalar(
+                out=result[:, a, :], in0=biased[:, a, :], scalar1=0.0, scalar2=0.0, op0=ALU.max, op1=ALU.add
+            )
+            nc.sync.dma_start(out=out[a * P : (a + 1) * P, :], in_=result[:, a, :])
+
+        for a in range(NODE_TILES):
+            nc.sync.dma_start(out=adj_sb[:, a, :], in_=adj[a * P : (a + 1) * P, :])
+        for half in range(2):
+            cols = slice(half * FEATS // 2, (half + 1) * FEATS // 2)
+            nc.sync.dma_start(out=x_sb[:, :, cols], in_=x[:, cols].rearrange("(t p) f -> p t f", p=P))
+        nc.sync.dma_start(out=w_sb[:], in_=W1.rearrange("(c p) f -> p c f", p=P))
+        nc.sync.dma_start(out=bias_sb[:], in_=b1.partition_broadcast(P))
+
+        make_identity(nc, ident_f32[:])
+        make_identity(nc, ident_bf16[:])
+        nc.vector.memset(warm[:], 1.0)
+        nc.scalar.activation(out=warm[:], in_=warm[:], func=ACT.Sqrt)
+
+        for pair in range(NODE_TILES // 2):
+            two = slice(2 * pair, 2 * pair + 2)
+            row_sum(2 * pair)
+            row_sum(2 * pair + 1)
+            nc.scalar.activation(out=root[:, two], in_=deg[:, two, 0], func=ACT.Sqrt, bias=EPS)
+        for pair in range(NODE_TILES // 2):
+            two = slice(2 * pair, 2 * pair + 2)
+            nc.vector.reciprocal(out=d_col[:, two], in_=root[:, two])
+            group_x(pair)
+        quantise(x_codes[:], x_scales[:], x_grouped[:].rearrange("p f t -> p (f t)"))
+
+        for a in range(NODE_TILES):
+            scale_and_transpose_rows(a)
+            if a >= 1:
+                transpose_w(a - 1)
+        for c in range(HIDDEN_TILES):
+            nc.scalar.copy(out=w_grouped[:, c], in_=banks["wT", c][:].rearrange("p t h -> p h t"))
+
+        for a in range(NODE_TILES + 1):
+            if a < NODE_TILES:
+                finish_norm_adj(a)
+            if a >= 1:
+                quantise(
+                    adj_codes[:, a - 1, :], adj_scales[:, a - 1, :], adj_grouped[:, a - 1].rearrange("p i t -> p (i t)")
+                )
+                first_matmul(a - 1)
+        for c in range(HIDDEN_TILES):
+            h_cols = slice(c * P, (c + 1) * P)
+            quantise(w_codes[:, h_cols], w_scales[:, h_cols], w_grouped[:, c].rearrange("p h t -> p (h t)"))
+
+        for a in range(NODE_TILES + 1):
+            if a < NODE_TILES:
+                quantise(agg_codes[:, a, :], agg_scales[:, a, :], agg_grouped[:, a].rearrange("p i t -> p (i t)"))
+                second_matmul(a)
+            if a >= 1:
+                finish_out(a - 1)

@@ -10,7 +10,6 @@ U8 = mybir.dt.uint8
 FP8X4 = mybir.dt.float8_e4m3fn_x4
 ACT = mybir.ActivationFunctionType
 ALU = mybir.AluOpType
-AXIS = mybir.AxisListType
 
 P = 128
 PACK = 4
@@ -39,7 +38,7 @@ def tile_simplegcn_pa_s_kernel(tc, x, adj, W1, b1, out):
         ident_f32 = keep.tile([P, P], F32)
         ident_bf16 = keep.tile([P, P], BF16)
         warm = keep.tile([P, 1], F32)
-        deg = keep.tile([P, NODE_TILES, 8], F32)
+        deg = keep.tile([P, NODE_TILES], F32)
         root = keep.tile([P, NODE_TILES], F32)
         d_col = keep.tile([P, NODE_TILES], F32)
         unread = keep.tile([P, NODE_TILES, NODES], BF16)
@@ -61,12 +60,15 @@ def tile_simplegcn_pa_s_kernel(tc, x, adj, W1, b1, out):
         banks = {}
 
         def row_sum(a):
-            if a % 2 == 0:
-                nc.vector.tensor_reduce(out=deg[:, a, 0:1], in_=adj_sb[:, a, :], axis=AXIS.X, op=ALU.add)
-            else:
-                nc.scalar.activation(
-                    out=unread[:, a, :], in_=adj_sb[:, a, :], func=ACT.Copy, accum_out=deg[:, a, 0:1]
-                )
+            nc.vector.tensor_scalar(
+                out=unread[:, a, :],
+                in0=adj_sb[:, a, :],
+                scalar1=1.0,
+                scalar2=None,
+                op0=ALU.mult,
+                op1=ALU.add,
+                accum_out=deg[:, a : a + 1],
+            )
 
         def group_x(half):
             cols = slice(half * FEATS // 2, (half + 1) * FEATS // 2)
@@ -128,9 +130,7 @@ def tile_simplegcn_pa_s_kernel(tc, x, adj, W1, b1, out):
 
         def finish_out(a):
             nc.vector.tensor_tensor(out=biased[:, a, :], in0=banks["out", a][:], in1=bias_sb[:], op=ALU.add)
-            nc.gpsimd.tensor_scalar(
-                out=result[:, a, :], in0=biased[:, a, :], scalar1=0.0, scalar2=0.0, op0=ALU.max, op1=ALU.add
-            )
+            nc.scalar.activation(out=result[:, a, :], in_=biased[:, a, :], func=ACT.Relu)
             nc.sync.dma_start(out=out[a * P : (a + 1) * P, :], in_=result[:, a, :])
 
         for a in range(NODE_TILES):
@@ -146,15 +146,13 @@ def tile_simplegcn_pa_s_kernel(tc, x, adj, W1, b1, out):
         nc.vector.memset(warm[:], 1.0)
         nc.scalar.activation(out=warm[:], in_=warm[:], func=ACT.Sqrt)
 
-        for pair in range(NODE_TILES // 2):
-            two = slice(2 * pair, 2 * pair + 2)
-            row_sum(2 * pair)
-            row_sum(2 * pair + 1)
-            nc.scalar.activation(out=root[:, two], in_=deg[:, two, 0], func=ACT.Sqrt, bias=EPS)
-        for pair in range(NODE_TILES // 2):
-            two = slice(2 * pair, 2 * pair + 2)
-            nc.vector.reciprocal(out=d_col[:, two], in_=root[:, two])
-            group_x(pair)
+        for a in range(NODE_TILES):
+            row_sum(a)
+        nc.scalar.activation(out=root[:], in_=deg[:], func=ACT.Sqrt, bias=EPS)
+        nc.vector.reciprocal(out=d_col[:], in_=root[:])
+
+        for half in range(2):
+            group_x(half)
         quantise(x_codes[:], x_scales[:], x_grouped[:].rearrange("p f t -> p (f t)"))
 
         for a in range(NODE_TILES):

@@ -20,6 +20,7 @@ EPS = 1e-8
 NODE_TILES = NODES // P
 HIDDEN_TILES = HIDDEN // P
 HIDDEN_PASSES = ((0, 256), (256, 128))
+OUT_LAG = 2
 
 FLOPS = 2 * NODES * NODES * FEATS + 2 * NODES * FEATS * HIDDEN
 
@@ -36,7 +37,6 @@ def tile_simplegcn_pa_s_kernel(tc, x, adj, W1, b1, out):
         w_sb = keep.tile([P, HIDDEN_TILES, FEATS], BF16)
         bias_sb = keep.tile([P, HIDDEN], BF16)
         ident_f32 = keep.tile([P, P], F32)
-        ident_bf16 = keep.tile([P, P], BF16)
         warm = keep.tile([P, 1], F32)
         deg = keep.tile([P, NODE_TILES], F32)
         root = keep.tile([P, NODE_TILES], F32)
@@ -70,9 +70,12 @@ def tile_simplegcn_pa_s_kernel(tc, x, adj, W1, b1, out):
                 accum_out=deg[:, a : a + 1],
             )
 
-        def group_x(half):
-            cols = slice(half * FEATS // 2, (half + 1) * FEATS // 2)
-            nc.vector.tensor_copy(out=x_grouped[:, cols, :], in_=x_sb[:, :, cols].rearrange("p t f -> p f t"))
+        def group_x(u):
+            cols = slice(u * FEATS // 2, (u + 1) * FEATS // 2)
+            nc.vector.tensor_copy(
+                out=x_grouped[:, cols, :].rearrange("p (e m) t -> p e m t", e=2),
+                in_=x_sb[:, :, cols].rearrange("p t (m e) -> p e m t", e=2),
+            )
 
         def quantise(codes, scales, grouped):
             nc.vector.quantize_mx(out=codes.bitcast(FP8X4), scales=scales, in_=grouped)
@@ -95,10 +98,17 @@ def tile_simplegcn_pa_s_kernel(tc, x, adj, W1, b1, out):
             )
 
         def transpose_w(c):
-            wT_ps = psum.tile([P, PACK, P], BF16, tag="bank")
-            for t in range(PACK):
-                nc.tensor.transpose(wT_ps[:, t, :], w_sb[:, c, t * P : (t + 1) * P], ident_bf16[:])
+            w_words = w_sb[:, c, :].bitcast(F32)
+            wT_ps = psum.tile([P, 2, P], F32, tag="bank")
+            for u in range(2):
+                nc.tensor.transpose(wT_ps[:, u, :], w_words[:, u * P : (u + 1) * P], ident_f32[:])
             banks["wT", c] = wT_ps
+
+        def group_w(c):
+            nc.scalar.copy(
+                out=w_grouped[:, c].rearrange("p h t -> p (h t)").bitcast(F32).rearrange("p (h u) -> p h u", u=2),
+                in_=banks["wT", c][:].rearrange("p u h -> p h u"),
+            )
 
         def first_matmul(a):
             aggT_ps = psum.tile([P, PACK, P], F32, tag="bank")
@@ -135,14 +145,13 @@ def tile_simplegcn_pa_s_kernel(tc, x, adj, W1, b1, out):
 
         for a in range(NODE_TILES):
             nc.sync.dma_start(out=adj_sb[:, a, :], in_=adj[a * P : (a + 1) * P, :])
-        for half in range(2):
-            cols = slice(half * FEATS // 2, (half + 1) * FEATS // 2)
+        for u in range(2):
+            cols = slice(u * FEATS // 2, (u + 1) * FEATS // 2)
             nc.sync.dma_start(out=x_sb[:, :, cols], in_=x[:, cols].rearrange("(t p) f -> p t f", p=P))
         nc.sync.dma_start(out=w_sb[:], in_=W1.rearrange("(c p) f -> p c f", p=P))
         nc.sync.dma_start(out=bias_sb[:], in_=b1.partition_broadcast(P))
 
         make_identity(nc, ident_f32[:])
-        make_identity(nc, ident_bf16[:])
         nc.vector.memset(warm[:], 1.0)
         nc.scalar.activation(out=warm[:], in_=warm[:], func=ACT.Sqrt)
 
@@ -151,21 +160,21 @@ def tile_simplegcn_pa_s_kernel(tc, x, adj, W1, b1, out):
         nc.scalar.activation(out=root[:], in_=deg[:], func=ACT.Sqrt, bias=EPS)
         nc.vector.reciprocal(out=d_col[:], in_=root[:])
 
-        for half in range(2):
-            group_x(half)
-        quantise(x_codes[:], x_scales[:], x_grouped[:].rearrange("p f t -> p (f t)"))
-
+        for u in range(2):
+            group_x(u)
         for a in range(NODE_TILES):
             scale_and_transpose_rows(a)
             if a >= 1:
                 transpose_w(a - 1)
         for c in range(HIDDEN_TILES):
-            nc.scalar.copy(out=w_grouped[:, c], in_=banks["wT", c][:].rearrange("p t h -> p h t"))
+            group_w(c)
 
         for a in range(NODE_TILES + 1):
             if a < NODE_TILES:
                 finish_norm_adj(a)
-            if a >= 1:
+            if a == 0:
+                quantise(x_codes[:], x_scales[:], x_grouped[:].rearrange("p f t -> p (f t)"))
+            else:
                 quantise(
                     adj_codes[:, a - 1, :], adj_scales[:, a - 1, :], adj_grouped[:, a - 1].rearrange("p i t -> p (i t)")
                 )
@@ -174,9 +183,9 @@ def tile_simplegcn_pa_s_kernel(tc, x, adj, W1, b1, out):
             h_cols = slice(c * P, (c + 1) * P)
             quantise(w_codes[:, h_cols], w_scales[:, h_cols], w_grouped[:, c].rearrange("p h t -> p (h t)"))
 
-        for a in range(NODE_TILES + 1):
+        for a in range(NODE_TILES + OUT_LAG):
             if a < NODE_TILES:
                 quantise(agg_codes[:, a, :], agg_scales[:, a, :], agg_grouped[:, a].rearrange("p i t -> p (i t)"))
                 second_matmul(a)
-            if a >= 1:
-                finish_out(a - 1)
+            if a >= OUT_LAG:
+                finish_out(a - OUT_LAG)

@@ -20,7 +20,6 @@ EPS = 1e-8
 NODE_TILES = NODES // P
 HIDDEN_TILES = HIDDEN // P
 HIDDEN_PASSES = ((0, 256), (256, 128))
-OUT_LAG = 2
 
 FLOPS = 2 * NODES * NODES * FEATS + 2 * NODES * FEATS * HIDDEN
 
@@ -39,10 +38,9 @@ def tile_simplegcn_pa_s_kernel(tc, x, adj, W1, b1, out):
         ident_f32 = keep.tile([P, P], F32)
         warm = keep.tile([P, 1], F32)
         deg = keep.tile([P, NODE_TILES], F32)
-        root = keep.tile([P, NODE_TILES], F32)
         d_col = keep.tile([P, NODE_TILES], F32)
         unread = keep.tile([P, NODE_TILES, NODES], BF16)
-        rows_scaled = keep.tile([P, NODE_TILES, NODES], F32)
+        norm_adj = keep.tile([P, NODE_TILES, NODES], BF16)
         x_grouped = keep.tile([P, FEATS, PACK], BF16, align_bytes=64)
         x_codes = keep.tile([P, FEATS], U32, align_bytes=64)
         x_scales = keep.tile([P, FEATS], U8, align_bytes=64)
@@ -70,9 +68,40 @@ def tile_simplegcn_pa_s_kernel(tc, x, adj, W1, b1, out):
                 accum_out=deg[:, a : a + 1],
             )
 
-        def group_x(u):
+        def spread_d():
+            d_row = psum.tile([P, NODES], F32, tag="bank")
+            for a in range(NODE_TILES):
+                nc.tensor.transpose(
+                    d_row[:, a * P : (a + 1) * P], d_col[:, a : a + 1].to_broadcast([P, P]), ident_f32[:]
+                )
+            banks["d_row"] = d_row
+
+        def normalise(a):
+            nc.vector.scalar_tensor_tensor(
+                out=norm_adj[:, a, :],
+                in0=adj_sb[:, a, :],
+                scalar=d_col[:, a : a + 1],
+                in1=banks["d_row"][:],
+                op0=ALU.mult,
+                op1=ALU.mult,
+            )
+
+        def transpose_pairs(rows, key):
+            words = rows.bitcast(F32)
+            turned = psum.tile([P, 2, P], F32, tag="bank")
+            for u in range(2):
+                nc.tensor.transpose(turned[:, u, :], words[:, u * P : (u + 1) * P], ident_f32[:])
+            banks[key] = turned
+
+        def group_pairs(grouped, key):
+            nc.scalar.copy(
+                out=grouped.rearrange("p h t -> p (h t)").bitcast(F32).rearrange("p (h u) -> p h u", u=2),
+                in_=banks[key][:].rearrange("p u h -> p h u"),
+            )
+
+        def group_x(copy, u):
             cols = slice(u * FEATS // 2, (u + 1) * FEATS // 2)
-            nc.vector.tensor_copy(
+            copy(
                 out=x_grouped[:, cols, :].rearrange("p (e m) t -> p e m t", e=2),
                 in_=x_sb[:, :, cols].rearrange("p t (m e) -> p e m t", e=2),
             )
@@ -80,35 +109,19 @@ def tile_simplegcn_pa_s_kernel(tc, x, adj, W1, b1, out):
         def quantise(codes, scales, grouped):
             nc.vector.quantize_mx(out=codes.bitcast(FP8X4), scales=scales, in_=grouped)
 
-        def scale_and_transpose_rows(a):
-            nc.scalar.activation(
-                out=rows_scaled[:, a, :], in_=adj_sb[:, a, :], func=ACT.Copy, scale=d_col[:, a : a + 1]
-            )
-            adjT_ps = psum.tile([P, PACK, P], F32, tag="bank")
-            for t in range(PACK):
-                nc.tensor.transpose(adjT_ps[:, t, :], rows_scaled[:, a, t * P : (t + 1) * P], ident_f32[:])
-            banks["adjT", a] = adjT_ps
+        def quantise_x(u):
+            cols = slice(u * FEATS // 2, (u + 1) * FEATS // 2)
+            quantise(x_codes[:, cols], x_scales[:, cols], x_grouped[:, cols, :].rearrange("p f t -> p (f t)"))
 
-        def finish_norm_adj(a):
-            nc.vector.tensor_tensor(
-                out=adj_grouped[:, a],
-                in0=banks["adjT", a][:].rearrange("p t i -> p i t"),
-                in1=d_col[:].unsqueeze(1).to_broadcast([P, P, PACK]),
-                op=ALU.mult,
-            )
+        def quantise_adj(a):
+            quantise(adj_codes[:, a, :], adj_scales[:, a, :], adj_grouped[:, a].rearrange("p i t -> p (i t)"))
 
-        def transpose_w(c):
-            w_words = w_sb[:, c, :].bitcast(F32)
-            wT_ps = psum.tile([P, 2, P], F32, tag="bank")
-            for u in range(2):
-                nc.tensor.transpose(wT_ps[:, u, :], w_words[:, u * P : (u + 1) * P], ident_f32[:])
-            banks["wT", c] = wT_ps
+        def quantise_w(c):
+            cols = slice(c * P, (c + 1) * P)
+            quantise(w_codes[:, cols], w_scales[:, cols], w_grouped[:, c].rearrange("p h t -> p (h t)"))
 
-        def group_w(c):
-            nc.scalar.copy(
-                out=w_grouped[:, c].rearrange("p h t -> p (h t)").bitcast(F32).rearrange("p (h u) -> p h u", u=2),
-                in_=banks["wT", c][:].rearrange("p u h -> p h u"),
-            )
+        def quantise_agg(a):
+            quantise(agg_codes[:, a, :], agg_scales[:, a, :], agg_grouped[:, a].rearrange("p i t -> p (i t)"))
 
         def first_matmul(a):
             aggT_ps = psum.tile([P, PACK, P], F32, tag="bank")
@@ -122,7 +135,10 @@ def tile_simplegcn_pa_s_kernel(tc, x, adj, W1, b1, out):
                     start=True,
                     stop=True,
                 )
-            nc.scalar.copy(out=agg_grouped[:, a], in_=aggT_ps[:].rearrange("p t i -> p i t"))
+            banks["aggT", a] = aggT_ps
+
+        def group_agg(copy, a):
+            copy(out=agg_grouped[:, a], in_=banks["aggT", a][:].rearrange("p t i -> p i t"))
 
         def second_matmul(a):
             out_ps = psum.tile([P, HIDDEN], F32, tag="bank")
@@ -145,47 +161,42 @@ def tile_simplegcn_pa_s_kernel(tc, x, adj, W1, b1, out):
 
         for a in range(NODE_TILES):
             nc.sync.dma_start(out=adj_sb[:, a, :], in_=adj[a * P : (a + 1) * P, :])
-        for u in range(2):
-            cols = slice(u * FEATS // 2, (u + 1) * FEATS // 2)
-            nc.sync.dma_start(out=x_sb[:, :, cols], in_=x[:, cols].rearrange("(t p) f -> p t f", p=P))
+        nc.sync.dma_start(out=x_sb[:].rearrange("p (u e) f -> p u e f", e=2), in_=x.rearrange("(u p e) f -> p u e f", p=P, e=2))
         nc.sync.dma_start(out=w_sb[:], in_=W1.rearrange("(c p) f -> p c f", p=P))
         nc.sync.dma_start(out=bias_sb[:], in_=b1.partition_broadcast(P))
 
         make_identity(nc, ident_f32[:])
         nc.vector.memset(warm[:], 1.0)
-        nc.scalar.activation(out=warm[:], in_=warm[:], func=ACT.Sqrt)
+        nc.scalar.activation(out=warm[:], in_=warm[:], func=ACT.Abs_reciprocal_sqrt)
 
         for a in range(NODE_TILES):
             row_sum(a)
-        nc.scalar.activation(out=root[:], in_=deg[:], func=ACT.Sqrt, bias=EPS)
-        nc.vector.reciprocal(out=d_col[:], in_=root[:])
+        nc.scalar.activation(out=d_col[:], in_=deg[:], func=ACT.Abs_reciprocal_sqrt, bias=EPS)
+        spread_d()
+
+        group_x(nc.vector.tensor_copy, 0)
+        group_x(nc.scalar.copy, 1)
+        for c in range(HIDDEN_TILES):
+            transpose_pairs(w_sb[:, c, :], ("wT", c))
+            group_pairs(w_grouped[:, c], ("wT", c))
+        for a in range(NODE_TILES):
+            normalise(a)
+            transpose_pairs(norm_adj[:, a, :], ("adjT", a))
+            group_pairs(adj_grouped[:, a], ("adjT", a))
 
         for u in range(2):
-            group_x(u)
+            quantise_x(u)
         for a in range(NODE_TILES):
-            scale_and_transpose_rows(a)
-            if a >= 1:
-                transpose_w(a - 1)
+            quantise_adj(a)
+            first_matmul(a)
         for c in range(HIDDEN_TILES):
-            group_w(c)
+            quantise_w(c)
+        for a in range(NODE_TILES):
+            group_agg(nc.vector.tensor_copy if a == 1 else nc.scalar.copy, a)
 
-        for a in range(NODE_TILES + 1):
+        for a in range(NODE_TILES + 2):
             if a < NODE_TILES:
-                finish_norm_adj(a)
-            if a == 0:
-                quantise(x_codes[:], x_scales[:], x_grouped[:].rearrange("p f t -> p (f t)"))
-            else:
-                quantise(
-                    adj_codes[:, a - 1, :], adj_scales[:, a - 1, :], adj_grouped[:, a - 1].rearrange("p i t -> p (i t)")
-                )
-                first_matmul(a - 1)
-        for c in range(HIDDEN_TILES):
-            h_cols = slice(c * P, (c + 1) * P)
-            quantise(w_codes[:, h_cols], w_scales[:, h_cols], w_grouped[:, c].rearrange("p h t -> p (h t)"))
-
-        for a in range(NODE_TILES + OUT_LAG):
-            if a < NODE_TILES:
-                quantise(agg_codes[:, a, :], agg_scales[:, a, :], agg_grouped[:, a].rearrange("p i t -> p (i t)"))
+                quantise_agg(a)
                 second_matmul(a)
-            if a >= OUT_LAG:
-                finish_out(a - OUT_LAG)
+            if a >= 2:
+                finish_out(a - 2)

@@ -34,7 +34,9 @@ def tile_simplegcn_pa_s_kernel(tc, x, adj, W1, b1, out):
         adj_sb = keep.tile([P, NODE_TILES, NODES], BF16)
         x_sb = keep.tile([P, PACK, FEATS], BF16)
         w_sb = keep.tile([P, HIDDEN_TILES, FEATS], BF16)
-        bias_sb = keep.tile([P, HIDDEN], BF16)
+        b_rows = keep.tile([P, HIDDEN], BF16)
+        ones = keep.tile([P, P], BF16)
+        bias_sb = keep.tile([P, HIDDEN], F32)
         ident_f32 = keep.tile([P, P], F32)
         warm = keep.tile([P, 1], F32)
         deg = keep.tile([P, NODE_TILES], F32)
@@ -154,6 +156,11 @@ def tile_simplegcn_pa_s_kernel(tc, x, adj, W1, b1, out):
                 )
             banks["out", a] = out_ps
 
+        def spread_bias():
+            bias_ps = psum.tile([P, HIDDEN], F32, tag="bank")
+            nc.tensor.matmul(bias_ps[:], lhsT=ones[:], rhs=b_rows[:], start=True, stop=True)
+            nc.scalar.copy(out=bias_sb[:], in_=bias_ps[:])
+
         def finish_out(a):
             nc.vector.tensor_tensor(out=biased[:, a, :], in0=banks["out", a][:], in1=bias_sb[:], op=ALU.add)
             nc.scalar.activation(out=result[:, a, :], in_=biased[:, a, :], func=ACT.Relu)
@@ -163,10 +170,12 @@ def tile_simplegcn_pa_s_kernel(tc, x, adj, W1, b1, out):
             nc.sync.dma_start(out=adj_sb[:, a, :], in_=adj[a * P : (a + 1) * P, :])
         nc.sync.dma_start(out=x_sb[:].rearrange("p (u e) f -> p u e f", e=2), in_=x.rearrange("(u p e) f -> p u e f", p=P, e=2))
         nc.sync.dma_start(out=w_sb[:], in_=W1.rearrange("(c p) f -> p c f", p=P))
-        nc.sync.dma_start(out=bias_sb[:], in_=b1.partition_broadcast(P))
+        nc.gpsimd.memset(b_rows[:], 0.0)
+        nc.sync.dma_start(out=b_rows[0:1, :], in_=b1.unsqueeze(0))
 
         make_identity(nc, ident_f32[:])
         nc.vector.memset(warm[:], 1.0)
+        nc.vector.memset(ones[:], 1.0)
         nc.scalar.activation(out=warm[:], in_=warm[:], func=ACT.Abs_reciprocal_sqrt)
 
         for a in range(NODE_TILES):
@@ -183,6 +192,7 @@ def tile_simplegcn_pa_s_kernel(tc, x, adj, W1, b1, out):
             normalise(a)
             transpose_pairs(norm_adj[:, a, :], ("adjT", a))
             group_pairs(adj_grouped[:, a], ("adjT", a))
+        spread_bias()
 
         for u in range(2):
             quantise_x(u)

@@ -29,13 +29,16 @@ def tile_simplegcn_pa_s_kernel(tc, x, adj, W1, b1, out):
     with ExitStack() as ctx:
         ctx.enter_context(tc.manual_schedule())
         keep = ctx.enter_context(tc.tile_pool(name="keep", bufs=1))
-        psum = ctx.enter_context(tc.psum_pool(name="psum", bufs=8))
+        psum = ctx.enter_context(tc.psum_pool(name="psum", bufs=7))
+        psum_keep = ctx.enter_context(tc.psum_pool(name="psum_keep", bufs=1))
 
         adj_sb = keep.tile([P, NODE_TILES, NODES], BF16)
         x_sb = keep.tile([P, PACK, FEATS], BF16)
         w_sb = keep.tile([P, HIDDEN_TILES, FEATS], BF16)
         b_rows = keep.tile([P, HIDDEN], BF16)
-        ones = keep.tile([P, P], BF16)
+        b_rows_f32 = keep.tile([P, HIDDEN], F32)
+        ones = keep.tile([P, P], F32)
+        zeros = keep.tile([P, P], F32)
         bias_sb = keep.tile([P, HIDDEN], F32)
         ident_f32 = keep.tile([P, P], F32)
         warm = keep.tile([P, 1], F32)
@@ -57,6 +60,7 @@ def tile_simplegcn_pa_s_kernel(tc, x, adj, W1, b1, out):
         agg_scales = keep.tile([P, NODE_TILES, P], U8, align_bytes=64)
         biased = keep.tile([P, NODE_TILES, HIDDEN], F32)
         result = keep.tile([P, NODE_TILES, HIDDEN], F32)
+        unread_ps = psum_keep.tile([P, P], F32)
         banks = {}
 
         def row_sum(a):
@@ -156,9 +160,13 @@ def tile_simplegcn_pa_s_kernel(tc, x, adj, W1, b1, out):
                 )
             banks["out", a] = out_ps
 
+        def keep_busy(count):
+            for n in range(count):
+                nc.tensor.matmul(unread_ps[:], lhsT=zeros[:], rhs=zeros[:], start=True, stop=True)
+
         def spread_bias():
             bias_ps = psum.tile([P, HIDDEN], F32, tag="bank")
-            nc.tensor.matmul(bias_ps[:], lhsT=ones[:], rhs=b_rows[:], start=True, stop=True)
+            nc.tensor.matmul(bias_ps[:], lhsT=ones[:], rhs=b_rows_f32[:], start=True, stop=True)
             nc.scalar.copy(out=bias_sb[:], in_=bias_ps[:])
 
         def finish_out(a):
@@ -175,7 +183,10 @@ def tile_simplegcn_pa_s_kernel(tc, x, adj, W1, b1, out):
 
         make_identity(nc, ident_f32[:])
         nc.vector.memset(warm[:], 1.0)
+        nc.vector.memset(zeros[:], 0.0)
         nc.vector.memset(ones[:], 1.0)
+        keep_busy(4)
+        nc.gpsimd.tensor_copy(out=b_rows_f32[:], in_=b_rows[:])
         nc.scalar.activation(out=warm[:], in_=warm[:], func=ACT.Abs_reciprocal_sqrt)
 
         for a in range(NODE_TILES):
@@ -190,6 +201,7 @@ def tile_simplegcn_pa_s_kernel(tc, x, adj, W1, b1, out):
             group_pairs(w_grouped[:, c], ("wT", c))
         for a in range(NODE_TILES):
             normalise(a)
+            keep_busy(1)
             transpose_pairs(norm_adj[:, a, :], ("adjT", a))
             group_pairs(adj_grouped[:, a], ("adjT", a))
         spread_bias()

@@ -29,15 +29,14 @@ def tile_simplegcn_pa_s_kernel(tc, x, adj, W1, b1, out):
     with ExitStack() as ctx:
         ctx.enter_context(tc.manual_schedule())
         keep = ctx.enter_context(tc.tile_pool(name="keep", bufs=1))
-        psum = ctx.enter_context(tc.psum_pool(name="psum", bufs=7))
+        psum = ctx.enter_context(tc.psum_pool(name="psum", bufs=6))
         psum_keep = ctx.enter_context(tc.psum_pool(name="psum_keep", bufs=1))
 
         adj_sb = keep.tile([P, NODE_TILES, NODES], BF16)
         x_sb = keep.tile([P, PACK, FEATS], BF16)
         w_sb = keep.tile([P, HIDDEN_TILES, FEATS], BF16)
         b_rows = keep.tile([P, HIDDEN], BF16)
-        b_rows_f32 = keep.tile([P, HIDDEN], F32)
-        ones = keep.tile([P, P], F32)
+        ones = keep.tile([P, P], BF16)
         zeros = keep.tile([P, P], F32)
         bias_sb = keep.tile([P, HIDDEN], F32)
         ident_f32 = keep.tile([P, P], F32)
@@ -60,6 +59,7 @@ def tile_simplegcn_pa_s_kernel(tc, x, adj, W1, b1, out):
         agg_scales = keep.tile([P, NODE_TILES, P], U8, align_bytes=64)
         biased = keep.tile([P, NODE_TILES, HIDDEN], F32)
         result = keep.tile([P, NODE_TILES, HIDDEN], F32)
+        d_row = psum_keep.tile([P, NODES], F32)
         unread_ps = psum_keep.tile([P, P], F32)
         banks = {}
 
@@ -74,20 +74,17 @@ def tile_simplegcn_pa_s_kernel(tc, x, adj, W1, b1, out):
                 accum_out=deg[:, a : a + 1],
             )
 
-        def spread_d():
-            d_row = psum.tile([P, NODES], F32, tag="bank")
-            for a in range(NODE_TILES):
-                nc.tensor.transpose(
-                    d_row[:, a * P : (a + 1) * P], d_col[:, a : a + 1].to_broadcast([P, P]), ident_f32[:]
-                )
-            banks["d_row"] = d_row
+        def finish_d(a):
+            column = d_col[:, a : a + 1]
+            nc.scalar.activation(out=column, in_=deg[:, a : a + 1], func=ACT.Abs_reciprocal_sqrt, bias=EPS)
+            nc.tensor.transpose(d_row[:, a * P : (a + 1) * P], column.to_broadcast([P, P]), ident_f32[:])
 
         def normalise(a):
             nc.vector.scalar_tensor_tensor(
                 out=norm_adj[:, a, :],
                 in0=adj_sb[:, a, :],
                 scalar=d_col[:, a : a + 1],
-                in1=banks["d_row"][:],
+                in1=d_row[:],
                 op0=ALU.mult,
                 op1=ALU.mult,
             )
@@ -105,12 +102,18 @@ def tile_simplegcn_pa_s_kernel(tc, x, adj, W1, b1, out):
                 in_=banks[key][:].rearrange("p u h -> p h u"),
             )
 
-        def group_x(copy, u):
+        def grouping_of_x(u):
             cols = slice(u * FEATS // 2, (u + 1) * FEATS // 2)
-            copy(
-                out=x_grouped[:, cols, :].rearrange("p (e m) t -> p e m t", e=2),
-                in_=x_sb[:, :, cols].rearrange("p t (m e) -> p e m t", e=2),
+            return (
+                x_grouped[:, cols, :].rearrange("p (e m) t -> p e m t", e=2),
+                x_sb[:, :, cols].rearrange("p t (m e) -> p e m t", e=2),
             )
+
+        def group_x():
+            grouped, rows = grouping_of_x(0)
+            nc.gpsimd.tensor_scalar(out=grouped, in0=rows, scalar1=1.0, scalar2=0.0, op0=ALU.mult, op1=ALU.add)
+            grouped, rows = grouping_of_x(1)
+            nc.scalar.copy(out=grouped, in_=rows)
 
         def quantise(codes, scales, grouped):
             nc.vector.quantize_mx(out=codes.bitcast(FP8X4), scales=scales, in_=grouped)
@@ -166,7 +169,7 @@ def tile_simplegcn_pa_s_kernel(tc, x, adj, W1, b1, out):
 
         def spread_bias():
             bias_ps = psum.tile([P, HIDDEN], F32, tag="bank")
-            nc.tensor.matmul(bias_ps[:], lhsT=ones[:], rhs=b_rows_f32[:], start=True, stop=True)
+            nc.tensor.matmul(bias_ps[:], lhsT=ones[:], rhs=b_rows[:], start=True, stop=True)
             nc.scalar.copy(out=bias_sb[:], in_=bias_ps[:])
 
         def finish_out(a):
@@ -176,7 +179,9 @@ def tile_simplegcn_pa_s_kernel(tc, x, adj, W1, b1, out):
 
         for a in range(NODE_TILES):
             nc.sync.dma_start(out=adj_sb[:, a, :], in_=adj[a * P : (a + 1) * P, :])
-        nc.sync.dma_start(out=x_sb[:].rearrange("p (u e) f -> p u e f", e=2), in_=x.rearrange("(u p e) f -> p u e f", p=P, e=2))
+        nc.sync.dma_start(
+            out=x_sb[:].rearrange("p (u e) f -> p u e f", e=2), in_=x.rearrange("(u p e) f -> p u e f", p=P, e=2)
+        )
         nc.sync.dma_start(out=w_sb[:], in_=W1.rearrange("(c p) f -> p c f", p=P))
         nc.gpsimd.memset(b_rows[:], 0.0)
         nc.sync.dma_start(out=b_rows[0:1, :], in_=b1.unsqueeze(0))
@@ -186,24 +191,22 @@ def tile_simplegcn_pa_s_kernel(tc, x, adj, W1, b1, out):
         nc.vector.memset(zeros[:], 0.0)
         nc.vector.memset(ones[:], 1.0)
         keep_busy(4)
-        nc.gpsimd.tensor_copy(out=b_rows_f32[:], in_=b_rows[:])
         nc.scalar.activation(out=warm[:], in_=warm[:], func=ACT.Abs_reciprocal_sqrt)
 
         for a in range(NODE_TILES):
             row_sum(a)
-        nc.scalar.activation(out=d_col[:], in_=deg[:], func=ACT.Abs_reciprocal_sqrt, bias=EPS)
-        spread_d()
+            finish_d(a)
 
-        group_x(nc.vector.tensor_copy, 0)
-        group_x(nc.scalar.copy, 1)
-        for c in range(HIDDEN_TILES):
-            transpose_pairs(w_sb[:, c, :], ("wT", c))
-            group_pairs(w_grouped[:, c], ("wT", c))
+        group_x()
         for a in range(NODE_TILES):
             normalise(a)
             keep_busy(1)
             transpose_pairs(norm_adj[:, a, :], ("adjT", a))
             group_pairs(adj_grouped[:, a], ("adjT", a))
+            if a == 0:
+                for c in range(HIDDEN_TILES):
+                    transpose_pairs(w_sb[:, c, :], ("wT", c))
+                    group_pairs(w_grouped[:, c], ("wT", c))
         spread_bias()
 
         for u in range(2):

@@ -17,6 +17,7 @@ NODES = 512
 FEATS = 512
 HIDDEN = 384
 EPS = 1e-8
+EARLY = 384
 NODE_TILES = NODES // P
 HIDDEN_TILES = HIDDEN // P
 HIDDEN_PASSES = ((0, 256), (256, 128))
@@ -60,7 +61,8 @@ def tile_simplegcn_pa_s_kernel(tc, x, adj, W1, b1, out):
         biased = keep.tile([P, NODE_TILES, HIDDEN], F32)
         result = keep.tile([P, NODE_TILES, HIDDEN], F32)
         d_row = psum_keep.tile([P, NODES], F32)
-        unread_ps = psum_keep.tile([P, P], F32)
+        early_ps = psum_keep.tile([P, NODES], F32)
+        unread_ps = early_ps[:, EARLY:NODES]
         banks = {}
 
         def row_sum(a):
@@ -77,14 +79,17 @@ def tile_simplegcn_pa_s_kernel(tc, x, adj, W1, b1, out):
         def finish_d(a):
             column = d_col[:, a : a + 1]
             nc.scalar.activation(out=column, in_=deg[:, a : a + 1], func=ACT.Abs_reciprocal_sqrt, bias=EPS)
-            nc.tensor.transpose(d_row[:, a * P : (a + 1) * P], column.to_broadcast([P, P]), ident_f32[:])
+            cols = slice(a * P, (a + 1) * P)
+            if cols.stop <= EARLY:
+                nc.tensor.transpose(early_ps[:, cols], column.to_broadcast([P, P]), ident_f32[:])
+            nc.tensor.transpose(d_row[:, cols], column.to_broadcast([P, P]), ident_f32[:])
 
-        def normalise(a):
+        def normalise(a, row, first, end):
             nc.vector.scalar_tensor_tensor(
-                out=norm_adj[:, a, :],
-                in0=adj_sb[:, a, :],
+                out=norm_adj[:, a, first:end],
+                in0=adj_sb[:, a, first:end],
                 scalar=d_col[:, a : a + 1],
-                in1=d_row[:],
+                in1=row[:, first:end],
                 op0=ALU.mult,
                 op1=ALU.mult,
             )
@@ -118,16 +123,16 @@ def tile_simplegcn_pa_s_kernel(tc, x, adj, W1, b1, out):
         def quantise(codes, scales, grouped):
             nc.vector.quantize_mx(out=codes.bitcast(FP8X4), scales=scales, in_=grouped)
 
-        def quantise_x(u):
-            cols = slice(u * FEATS // 2, (u + 1) * FEATS // 2)
-            quantise(x_codes[:, cols], x_scales[:, cols], x_grouped[:, cols, :].rearrange("p f t -> p (f t)"))
+        def quantise_x():
+            quantise(x_codes[:], x_scales[:], x_grouped[:].rearrange("p f t -> p (f t)"))
 
         def quantise_adj(a):
             quantise(adj_codes[:, a, :], adj_scales[:, a, :], adj_grouped[:, a].rearrange("p i t -> p (i t)"))
 
-        def quantise_w(c):
-            cols = slice(c * P, (c + 1) * P)
-            quantise(w_codes[:, cols], w_scales[:, cols], w_grouped[:, c].rearrange("p h t -> p (h t)"))
+        def quantise_w(first, width):
+            cols = slice(first, first + width)
+            grouped = w_grouped[:].rearrange("p c h t -> p (c h t)")[:, first * PACK : (first + width) * PACK]
+            quantise(w_codes[:, cols], w_scales[:, cols], grouped)
 
         def quantise_agg(a):
             quantise(agg_codes[:, a, :], agg_scales[:, a, :], agg_grouped[:, a].rearrange("p i t -> p (i t)"))
@@ -165,7 +170,7 @@ def tile_simplegcn_pa_s_kernel(tc, x, adj, W1, b1, out):
 
         def keep_busy(count):
             for n in range(count):
-                nc.tensor.matmul(unread_ps[:], lhsT=zeros[:], rhs=zeros[:], start=True, stop=True)
+                nc.tensor.matmul(unread_ps, lhsT=zeros[:], rhs=zeros[:], start=True, stop=True)
 
         def spread_bias():
             bias_ps = psum.tile([P, HIDDEN], F32, tag="bank")
@@ -199,23 +204,25 @@ def tile_simplegcn_pa_s_kernel(tc, x, adj, W1, b1, out):
 
         group_x()
         for a in range(NODE_TILES):
-            normalise(a)
+            if a == 0:
+                normalise(a, early_ps, 0, EARLY)
+                normalise(a, d_row, EARLY, NODES)
+            else:
+                normalise(a, d_row, 0, NODES)
             keep_busy(1)
             transpose_pairs(norm_adj[:, a, :], ("adjT", a))
             group_pairs(adj_grouped[:, a], ("adjT", a))
-            if a == 0:
-                for c in range(HIDDEN_TILES):
-                    transpose_pairs(w_sb[:, c, :], ("wT", c))
-                    group_pairs(w_grouped[:, c], ("wT", c))
+            if a < HIDDEN_TILES:
+                transpose_pairs(w_sb[:, a, :], ("wT", a))
+                group_pairs(w_grouped[:, a], ("wT", a))
         spread_bias()
 
-        for u in range(2):
-            quantise_x(u)
+        quantise_x()
         for a in range(NODE_TILES):
             quantise_adj(a)
             first_matmul(a)
-        for c in range(HIDDEN_TILES):
-            quantise_w(c)
+        for first, width in HIDDEN_PASSES:
+            quantise_w(first, width)
         for a in range(NODE_TILES):
             group_agg(nc.vector.tensor_copy if a == 1 else nc.scalar.copy, a)
 

@@ -30,7 +30,7 @@ def tile_simplegcn_pa_s_kernel(tc, x, adj, W1, b1, out):
     with ExitStack() as ctx:
         ctx.enter_context(tc.manual_schedule())
         keep = ctx.enter_context(tc.tile_pool(name="keep", bufs=1))
-        psum = ctx.enter_context(tc.psum_pool(name="psum", bufs=6))
+        psum = ctx.enter_context(tc.psum_pool(name="psum", bufs=5))
         psum_keep = ctx.enter_context(tc.psum_pool(name="psum_keep", bufs=1))
 
         adj_sb = keep.tile([P, NODE_TILES, NODES], BF16)
@@ -61,8 +61,8 @@ def tile_simplegcn_pa_s_kernel(tc, x, adj, W1, b1, out):
         biased = keep.tile([P, NODE_TILES, HIDDEN], F32)
         result = keep.tile([P, NODE_TILES, HIDDEN], F32)
         d_row = psum_keep.tile([P, NODES], F32)
-        early_ps = psum_keep.tile([P, NODES], F32)
-        unread_ps = early_ps[:, EARLY:NODES]
+        early_ps = psum_keep.tile([P, EARLY], F32)
+        unread_ps = psum_keep.tile([P, P], F32)
         banks = {}
 
         def row_sum(a):
@@ -170,7 +170,7 @@ def tile_simplegcn_pa_s_kernel(tc, x, adj, W1, b1, out):
 
         def keep_busy(count):
             for n in range(count):
-                nc.tensor.matmul(unread_ps, lhsT=zeros[:], rhs=zeros[:], start=True, stop=True)
+                nc.tensor.matmul(unread_ps[:], lhsT=zeros[:], rhs=zeros[:], start=True, stop=True)
 
         def spread_bias():
             bias_ps = psum.tile([P, HIDDEN], F32, tag="bank")
@@ -219,10 +219,10 @@ def tile_simplegcn_pa_s_kernel(tc, x, adj, W1, b1, out):
 
         quantise_x()
         for a in range(NODE_TILES):
+            if a >= 2:
+                quantise_w(*HIDDEN_PASSES[a - 2])
             quantise_adj(a)
             first_matmul(a)
-        for first, width in HIDDEN_PASSES:
-            quantise_w(first, width)
         for a in range(NODE_TILES):
             group_agg(nc.vector.tensor_copy if a == 1 else nc.scalar.copy, a)
 

@@ -17,7 +17,8 @@ NODES = 512
 FEATS = 512
 HIDDEN = 384
 EPS = 1e-8
-EARLY = 384
+EARLY = 256
+EARLY_TILES = 2
 NODE_TILES = NODES // P
 HIDDEN_TILES = HIDDEN // P
 HIDDEN_PASSES = ((0, 256), (256, 128))
@@ -36,10 +37,8 @@ def tile_simplegcn_pa_s_kernel(tc, x, adj, W1, b1, out):
         adj_sb = keep.tile([P, NODE_TILES, NODES], BF16)
         x_sb = keep.tile([P, PACK, FEATS], BF16)
         w_sb = keep.tile([P, HIDDEN_TILES, FEATS], BF16)
-        b_rows = keep.tile([P, HIDDEN], BF16)
-        ones = keep.tile([P, P], BF16)
         zeros = keep.tile([P, P], F32)
-        bias_sb = keep.tile([P, HIDDEN], F32)
+        bias_sb = keep.tile([P, HIDDEN], BF16)
         ident_f32 = keep.tile([P, P], F32)
         warm = keep.tile([P, 1], F32)
         deg = keep.tile([P, NODE_TILES], F32)
@@ -172,11 +171,6 @@ def tile_simplegcn_pa_s_kernel(tc, x, adj, W1, b1, out):
             for n in range(count):
                 nc.tensor.matmul(unread_ps[:], lhsT=zeros[:], rhs=zeros[:], start=True, stop=True)
 
-        def spread_bias():
-            bias_ps = psum.tile([P, HIDDEN], F32, tag="bank")
-            nc.tensor.matmul(bias_ps[:], lhsT=ones[:], rhs=b_rows[:], start=True, stop=True)
-            nc.scalar.copy(out=bias_sb[:], in_=bias_ps[:])
-
         def finish_out(a):
             nc.vector.tensor_tensor(out=biased[:, a, :], in0=banks["out", a][:], in1=bias_sb[:], op=ALU.add)
             nc.scalar.activation(out=result[:, a, :], in_=biased[:, a, :], func=ACT.Relu)
@@ -188,34 +182,32 @@ def tile_simplegcn_pa_s_kernel(tc, x, adj, W1, b1, out):
             out=x_sb[:].rearrange("p (u e) f -> p u e f", e=2), in_=x.rearrange("(u p e) f -> p u e f", p=P, e=2)
         )
         nc.sync.dma_start(out=w_sb[:], in_=W1.rearrange("(c p) f -> p c f", p=P))
-        nc.gpsimd.memset(b_rows[:], 0.0)
-        nc.sync.dma_start(out=b_rows[0:1, :], in_=b1.unsqueeze(0))
+        nc.sync.dma_start(out=bias_sb[:], in_=b1.partition_broadcast(P))
 
         make_identity(nc, ident_f32[:])
         nc.vector.memset(warm[:], 1.0)
         nc.vector.memset(zeros[:], 0.0)
-        nc.vector.memset(ones[:], 1.0)
         keep_busy(4)
         nc.scalar.activation(out=warm[:], in_=warm[:], func=ACT.Abs_reciprocal_sqrt)
 
         for a in range(NODE_TILES):
             row_sum(a)
             finish_d(a)
+            if a == 1:
+                keep_busy(1)
 
         group_x()
+        for a in range(EARLY_TILES):
+            normalise(a, early_ps, 0, EARLY)
         for a in range(NODE_TILES):
-            if a == 0:
-                normalise(a, early_ps, 0, EARLY)
-                normalise(a, d_row, EARLY, NODES)
-            else:
-                normalise(a, d_row, 0, NODES)
-            keep_busy(1)
+            normalise(a, d_row, EARLY if a < EARLY_TILES else 0, NODES)
+            keep_busy(2 if a == 0 else 1)
             transpose_pairs(norm_adj[:, a, :], ("adjT", a))
             group_pairs(adj_grouped[:, a], ("adjT", a))
             if a < HIDDEN_TILES:
                 transpose_pairs(w_sb[:, a, :], ("wT", a))
                 group_pairs(w_grouped[:, a], ("wT", a))
-        spread_bias()
+        keep_busy(1)
 
         quantise_x()
         for a in range(NODE_TILES):

@@ -172,7 +172,12 @@ def tile_simplegcn_pa_s_kernel(tc, x, adj, W1, b1, out):
                 nc.tensor.matmul(unread_ps[:], lhsT=zeros[:], rhs=zeros[:], start=True, stop=True)
 
         def finish_out(a):
-            nc.vector.tensor_tensor(out=biased[:, a, :], in0=banks["out", a][:], in1=bias_sb[:], op=ALU.add)
+            nc.vector.tensor_tensor(
+                out=biased[:, a, :].rearrange("p (m c) -> p m c", c=HIDDEN_TILES),
+                in0=banks["out", a][:].rearrange("p (c m) -> p m c", c=HIDDEN_TILES),
+                in1=bias_sb[:].rearrange("p (m c) -> p m c", c=HIDDEN_TILES),
+                op=ALU.add,
+            )
             nc.scalar.activation(out=result[:, a, :], in_=biased[:, a, :], func=ACT.Relu)
             nc.sync.dma_start(out=out[a * P : (a + 1) * P, :], in_=result[:, a, :])
 
@@ -181,7 +186,7 @@ def tile_simplegcn_pa_s_kernel(tc, x, adj, W1, b1, out):
         nc.sync.dma_start(
             out=x_sb[:].rearrange("p (u e) f -> p u e f", e=2), in_=x.rearrange("(u p e) f -> p u e f", p=P, e=2)
         )
-        nc.sync.dma_start(out=w_sb[:], in_=W1.rearrange("(c p) f -> p c f", p=P))
+        nc.sync.dma_start(out=w_sb[:], in_=W1.rearrange("(p c) f -> p c f", c=HIDDEN_TILES))
         nc.sync.dma_start(out=bias_sb[:], in_=b1.partition_broadcast(P))
 
         make_identity(nc, ident_f32[:])
@@ -204,17 +209,18 @@ def tile_simplegcn_pa_s_kernel(tc, x, adj, W1, b1, out):
             keep_busy(2 if a == 0 else 1)
             transpose_pairs(norm_adj[:, a, :], ("adjT", a))
             group_pairs(adj_grouped[:, a], ("adjT", a))
-            if a < HIDDEN_TILES:
-                transpose_pairs(w_sb[:, a, :], ("wT", a))
-                group_pairs(w_grouped[:, a], ("wT", a))
+            if a > 0:
+                transpose_pairs(w_sb[:, a - 1, :], ("wT", a - 1))
+                group_pairs(w_grouped[:, a - 1], ("wT", a - 1))
         keep_busy(1)
 
         quantise_x()
         for a in range(NODE_TILES):
-            if a >= 2:
-                quantise_w(*HIDDEN_PASSES[a - 2])
+            if a == 2:
+                quantise_w(*HIDDEN_PASSES[0])
             quantise_adj(a)
             first_matmul(a)
+        quantise_w(*HIDDEN_PASSES[1])
         for a in range(NODE_TILES):
             group_agg(nc.vector.tensor_copy if a == 1 else nc.scalar.copy, a)
 

@@ -117,7 +117,11 @@ def tile_simplegcn_pa_s_kernel(tc, x, adj, W1, b1, out):
             grouped, rows = grouping_of_x(0)
             nc.gpsimd.tensor_scalar(out=grouped, in0=rows, scalar1=1.0, scalar2=0.0, op0=ALU.mult, op1=ALU.add)
             grouped, rows = grouping_of_x(1)
-            nc.scalar.copy(out=grouped, in_=rows)
+            for e in range(2):
+                nc.scalar.copy(
+                    out=grouped[:, e].rearrange("p (c i) t -> p c t i", i=4),
+                    in_=rows[:, e].rearrange("p (c i) t -> p c t i", i=4),
+                )
 
         def quantise(codes, scales, grouped):
             nc.vector.quantize_mx(out=codes.bitcast(FP8X4), scales=scales, in_=grouped)
@@ -187,7 +191,6 @@ def tile_simplegcn_pa_s_kernel(tc, x, adj, W1, b1, out):
             out=x_sb[:].rearrange("p (u e) f -> p u e f", e=2), in_=x.rearrange("(u p e) f -> p u e f", p=P, e=2)
         )
         nc.sync.dma_start(out=w_sb[:], in_=W1.rearrange("(p c) f -> p c f", c=HIDDEN_TILES))
-        nc.sync.dma_start(out=bias_sb[:], in_=b1.partition_broadcast(P))
 
         make_identity(nc, ident_f32[:])
         nc.vector.memset(warm[:], 1.0)
@@ -202,6 +205,7 @@ def tile_simplegcn_pa_s_kernel(tc, x, adj, W1, b1, out):
                 keep_busy(1)
 
         group_x()
+        nc.scalar.dma_start(out=bias_sb[:], in_=b1.partition_broadcast(P))
         for a in range(EARLY_TILES):
             normalise(a, early_ps, 0, EARLY)
         for a in range(NODE_TILES):

from contextlib import ExitStack

from concourse import mybir
from concourse.masks import make_identity

F32 = mybir.dt.float32
BF16 = mybir.dt.bfloat16
U32 = mybir.dt.uint32
U8 = mybir.dt.uint8
FP8X4 = mybir.dt.float8_e4m3fn_x4
ACT = mybir.ActivationFunctionType
ALU = mybir.AluOpType

P = 128
PACK = 4
NODES = 512
FEATS = 512
HIDDEN = 384
EPS = 1e-8
EARLY = 256
EARLY_TILES = 2
NODE_TILES = NODES // P
HIDDEN_TILES = HIDDEN // P
HIDDEN_PASSES = ((0, 256), (256, 128))

FLOPS = 2 * NODES * NODES * FEATS + 2 * NODES * FEATS * HIDDEN


def tile_simplegcn_pa_s_kernel(tc, x, adj, W1, b1, out):
    nc = tc.nc
    with ExitStack() as ctx:
        ctx.enter_context(tc.manual_schedule())
        keep = ctx.enter_context(tc.tile_pool(name="keep", bufs=1))
        psum = ctx.enter_context(tc.psum_pool(name="psum", bufs=5))
        psum_keep = ctx.enter_context(tc.psum_pool(name="psum_keep", bufs=1))

        adj_sb = keep.tile([P, NODE_TILES, NODES], BF16)
        x_sb = keep.tile([P, PACK, FEATS], BF16)
        w_sb = keep.tile([P, HIDDEN_TILES, FEATS], BF16)
        zeros = keep.tile([P, P], F32)
        bias_sb = keep.tile([P, HIDDEN], BF16)
        ident_f32 = keep.tile([P, P], F32)
        warm = keep.tile([P, 1], F32)
        deg = keep.tile([P, NODE_TILES], F32)
        d_col = keep.tile([P, NODE_TILES], F32)
        unread = keep.tile([P, NODE_TILES, NODES], BF16)
        norm_adj = keep.tile([P, NODE_TILES, NODES], BF16)
        x_grouped = keep.tile([P, FEATS, PACK], BF16, align_bytes=64)
        x_codes = keep.tile([P, FEATS], U32, align_bytes=64)
        x_scales = keep.tile([P, FEATS], U8, align_bytes=64)
        adj_grouped = keep.tile([P, NODE_TILES, P, PACK], BF16, align_bytes=64)
        adj_codes = keep.tile([P, NODE_TILES, P], U32, align_bytes=64)
        adj_scales = keep.tile([P, NODE_TILES, P], U8, align_bytes=64)
        w_grouped = keep.tile([P, HIDDEN_TILES, P, PACK], BF16, align_bytes=64)
        w_codes = keep.tile([P, HIDDEN], U32, align_bytes=64)
        w_scales = keep.tile([P, HIDDEN], U8, align_bytes=64)
        agg_grouped = keep.tile([P, NODE_TILES, P, PACK], BF16, align_bytes=64)
        agg_codes = keep.tile([P, NODE_TILES, P], U32, align_bytes=64)
        agg_scales = keep.tile([P, NODE_TILES, P], U8, align_bytes=64)
        biased = keep.tile([P, NODE_TILES, HIDDEN], F32)
        result = keep.tile([P, NODE_TILES, HIDDEN], F32)
        d_row = psum_keep.tile([P, NODES], F32)
        early_ps = psum_keep.tile([P, EARLY], F32)
        unread_ps = psum_keep.tile([P, P], F32)
        banks = {}

        def row_sum(a):
            nc.vector.tensor_scalar(
                out=unread[:, a, :],
                in0=adj_sb[:, a, :],
                scalar1=1.0,
                scalar2=None,
                op0=ALU.mult,
                op1=ALU.add,
                accum_out=deg[:, a : a + 1],
            )

        def finish_d(a):
            column = d_col[:, a : a + 1]
            nc.scalar.activation(out=column, in_=deg[:, a : a + 1], func=ACT.Abs_reciprocal_sqrt, bias=EPS)
            cols = slice(a * P, (a + 1) * P)
            if cols.stop <= EARLY:
                nc.tensor.transpose(early_ps[:, cols], column.to_broadcast([P, P]), ident_f32[:])
            nc.tensor.transpose(d_row[:, cols], column.to_broadcast([P, P]), ident_f32[:])

        def normalise(a, row, first, end):
            nc.vector.scalar_tensor_tensor(
                out=norm_adj[:, a, first:end],
                in0=adj_sb[:, a, first:end],
                scalar=d_col[:, a : a + 1],
                in1=row[:, first:end],
                op0=ALU.mult,
                op1=ALU.mult,
            )

        def transpose_pairs(rows, key):
            words = rows.bitcast(F32)
            turned = psum.tile([P, 2, P], F32, tag="bank")
            for u in range(2):
                nc.tensor.transpose(turned[:, u, :], words[:, u * P : (u + 1) * P], ident_f32[:])
            banks[key] = turned

        def group_pairs(grouped, key):
            nc.scalar.copy(
                out=grouped.rearrange("p h t -> p (h t)").bitcast(F32).rearrange("p (h u) -> p h u", u=2),
                in_=banks[key][:].rearrange("p u h -> p h u"),
            )

        def grouping_of_x(u):
            cols = slice(u * FEATS // 2, (u + 1) * FEATS // 2)
            return (
                x_grouped[:, cols, :].rearrange("p (e m) t -> p e m t", e=2),
                x_sb[:, :, cols].rearrange("p t (m e) -> p e m t", e=2),
            )

        def group_x():
            grouped, rows = grouping_of_x(0)
            nc.gpsimd.tensor_scalar(out=grouped, in0=rows, scalar1=1.0, scalar2=0.0, op0=ALU.mult, op1=ALU.add)
            grouped, rows = grouping_of_x(1)
            for e in range(2):
                nc.scalar.copy(
                    out=grouped[:, e].rearrange("p (c i) t -> p c t i", i=4),
                    in_=rows[:, e].rearrange("p (c i) t -> p c t i", i=4),
                )

        def quantise(codes, scales, grouped):
            nc.vector.quantize_mx(out=codes.bitcast(FP8X4), scales=scales, in_=grouped)

        def quantise_x():
            quantise(x_codes[:], x_scales[:], x_grouped[:].rearrange("p f t -> p (f t)"))

        def quantise_adj(a):
            quantise(adj_codes[:, a, :], adj_scales[:, a, :], adj_grouped[:, a].rearrange("p i t -> p (i t)"))

        def quantise_w(first, width):
            cols = slice(first, first + width)
            grouped = w_grouped[:].rearrange("p c h t -> p (c h t)")[:, first * PACK : (first + width) * PACK]
            quantise(w_codes[:, cols], w_scales[:, cols], grouped)

        def quantise_agg(a):
            quantise(agg_codes[:, a, :], agg_scales[:, a, :], agg_grouped[:, a].rearrange("p i t -> p (i t)"))

        def first_matmul(a):
            aggT_ps = psum.tile([P, PACK, P], F32, tag="bank")
            for t in range(PACK):
                nc.tensor.matmul_mx(
                    out=aggT_ps[:, t, :],
                    lhsT=x_codes[:, t * P : (t + 1) * P].bitcast(FP8X4),
                    lhsT_scale=x_scales[:, t * P : (t + 1) * P],
                    rhs=adj_codes[:, a, :].bitcast(FP8X4),
                    rhs_scale=adj_scales[:, a, :],
                    start=True,
                    stop=True,
                )
            banks["aggT", a] = aggT_ps

        def group_agg(copy, a):
            copy(out=agg_grouped[:, a], in_=banks["aggT", a][:].rearrange("p t i -> p i t"))

        def second_matmul(a):
            out_ps = psum.tile([P, HIDDEN], F32, tag="bank")
            for first, width in HIDDEN_PASSES:
                nc.tensor.matmul_mx(
                    out=out_ps[:, first : first + width],
                    lhsT=agg_codes[:, a, :].bitcast(FP8X4),
                    lhsT_scale=agg_scales[:, a, :],
                    rhs=w_codes[:, first : first + width].bitcast(FP8X4),
                    rhs_scale=w_scales[:, first : first + width],
                    start=True,
                    stop=True,
                )
            banks["out", a] = out_ps

        def keep_busy(count):
            for n in range(count):
                nc.tensor.matmul(unread_ps[:], lhsT=zeros[:], rhs=zeros[:], start=True, stop=True)

        def finish_out(a):
            nc.vector.tensor_tensor(
                out=biased[:, a, :].rearrange("p (m c) -> p m c", c=HIDDEN_TILES),
                in0=banks["out", a][:].rearrange("p (c m) -> p m c", c=HIDDEN_TILES),
                in1=bias_sb[:].rearrange("p (m c) -> p m c", c=HIDDEN_TILES),
                op=ALU.add,
            )
            nc.scalar.activation(out=result[:, a, :], in_=biased[:, a, :], func=ACT.Relu)
            nc.sync.dma_start(out=out[a * P : (a + 1) * P, :], in_=result[:, a, :])

        for a in range(NODE_TILES):
            nc.sync.dma_start(out=adj_sb[:, a, :], in_=adj[a * P : (a + 1) * P, :])
        nc.sync.dma_start(
            out=x_sb[:].rearrange("p (u e) f -> p u e f", e=2), in_=x.rearrange("(u p e) f -> p u e f", p=P, e=2)
        )
        nc.sync.dma_start(out=w_sb[:], in_=W1.rearrange("(p c) f -> p c f", c=HIDDEN_TILES))

        make_identity(nc, ident_f32[:])
        nc.vector.memset(warm[:], 1.0)
        nc.vector.memset(zeros[:], 0.0)
        keep_busy(4)
        nc.scalar.activation(out=warm[:], in_=warm[:], func=ACT.Abs_reciprocal_sqrt)

        for a in range(NODE_TILES):
            row_sum(a)
            finish_d(a)
            if a == 1:
                keep_busy(1)

        group_x()
        nc.scalar.dma_start(out=bias_sb[:], in_=b1.partition_broadcast(P))
        for a in range(EARLY_TILES):
            normalise(a, early_ps, 0, EARLY)
        for a in range(NODE_TILES):
            normalise(a, d_row, EARLY if a < EARLY_TILES else 0, NODES)
            keep_busy(2 if a == 0 else 1)
            transpose_pairs(norm_adj[:, a, :], ("adjT", a))
            group_pairs(adj_grouped[:, a], ("adjT", a))
            if a > 0:
                transpose_pairs(w_sb[:, a - 1, :], ("wT", a - 1))
                group_pairs(w_grouped[:, a - 1], ("wT", a - 1))
        keep_busy(1)

        quantise_x()
        for a in range(NODE_TILES):
            if a == 2:
                quantise_w(*HIDDEN_PASSES[0])
            quantise_adj(a)
            first_matmul(a)
        quantise_w(*HIDDEN_PASSES[1])
        for a in range(NODE_TILES):
            group_agg(nc.vector.tensor_copy if a == 1 else nc.scalar.copy, a)

        for a in range(NODE_TILES + 2):
            if a < NODE_TILES:
                quantise_agg(a)
                second_matmul(a)
            if a >= 2:
                finish_out(a - 2)
